import numpy as np
import ml_dtypes


def mxq(x, axis, fmt="e4m3"):
    dtype, down = {"e4m3": (ml_dtypes.float8_e4m3fn, 7), "e5m2": (ml_dtypes.float8_e5m2, 14)}[fmt]
    v = np.moveaxis(np.asarray(x, np.float32).astype(ml_dtypes.bfloat16).astype(np.float64), axis, -1)
    blocks = v.reshape(v.shape[:-1] + (-1, 32))
    amax = np.abs(blocks).max(-1, keepdims=True)
    byte = np.maximum(np.where(amax > 0, np.frexp(amax)[1] - 1 + 127, 0) - down, 1)
    scale = np.exp2(byte - 127.0)
    codes = (blocks / scale).astype(np.float32).astype(dtype).astype(np.float64)
    return np.moveaxis((codes * scale).reshape(v.shape), -1, axis)


WIDE = False


def mx_kscale(k):
    if not WIDE:
        return np.ones(k)
    levels = np.array([10, -10, 5, -5, 0])
    if k % 512:
        return np.exp2(np.random.permutation(np.resize(levels, k // 32))).repeat(32)
    a = np.empty((k // 512, 16))
    for p in range(k // 512):
        a[p, :8] = np.random.permutation(np.resize(levels, 8))
        for g in range(8):
            far = levels[np.abs(levels - a[p, g]) >= 10]
            a[p, g + 8] = far[np.random.randint(len(far))]
    return np.exp2(a.ravel()).repeat(32)


BF16 = ml_dtypes.bfloat16


def bf(x):
    return np.asarray(x, np.float32).astype(BF16)


def f64(x):
    return np.asarray(x).astype(np.float64)


B, F, M, N, H, O = 1, 128, 32, 128, 512, 128
BN_EPS = 1e-5


def bn(x, g, b, m, v):
    sh = [1] * x.ndim
    sh[1] = -1
    return g.reshape(sh) * (x - m.reshape(sh)) * (1.0 / np.sqrt(v.reshape(sh) + BN_EPS)) + b.reshape(sh)


def draw0():
    s = mx_kscale(H)
    k = mx_kscale(H)
    return {"h2": bf(np.maximum(np.random.standard_normal((B, H, M, N)), 0.0) * s[None, :, None, None]),
            "W3": bf(np.random.standard_normal((H, H)) * 1.4 / np.sqrt(H) / s[None, :]),
            "g3": bf((1.0 + 0.1 * np.random.standard_normal(H)) * k),
            "b3": bf(0.2 * np.random.standard_normal(H) * k),
            "m3": bf(0.2 * np.random.standard_normal(H)),
            "v3": bf(np.random.uniform(0.5, 1.5, H)),
            "Wc1": bf(np.random.standard_normal((H, H)) * 0.4 / np.sqrt(H) / k[None, :]),
            "gc1": bf(1.0 + 0.1 * np.random.standard_normal(H)),
            "bc1": bf(0.2 * np.random.standard_normal(H)),
            "mc1": bf(0.2 * np.random.standard_normal(H)),
            "vc1": bf(np.random.uniform(0.5, 1.5, H))}


def core(h2, W3, g3, b3, m3, v3, Wc1, gc1, bc1, mc1, vc1):
    x3 = (mxq(f64(W3), 1, "e4m3") @ mxq(f64(h2).reshape(B, H, M * N), 1, "e4m3")).reshape(B, H, M, N)
    h3 = np.maximum(bn(x3, f64(g3), f64(b3), f64(m3), f64(v3)), 0.0)
    p = h3.max(axis=2)
    xc = mxq(f64(Wc1), 1, "e4m3") @ mxq(p, 1, "e4m3")
    return np.maximum(bn(xc, f64(gc1), f64(bc1), f64(mc1), f64(vc1)), 0.0)


def e4m3fn_bytes(y):
    return np.clip(np.asarray(y, np.float64), -448.0, 448.0).astype(np.float32).astype(ml_dtypes.float8_e4m3fn).view(np.uint8)


def e4m3fn_values(b):
    return np.asarray(b, np.uint8).view(ml_dtypes.float8_e4m3fn).astype(np.float64)


def setup_inputs():
    d = draw0()
    x0 = np.asarray(d['h2']).astype(np.float64)
    s = (np.max(np.abs(x0), axis=(0, 2, 3), keepdims=True) / 448.0).astype(np.float32)
    out = {}
    for k, v in d.items():
        if k == 'h2':
            out['h2_bytes'] = e4m3fn_bytes(x0 / s.astype(np.float64))
            out['h2_scale'] = s
        else:
            out[k] = v
    return out


def reference(h2_bytes, h2_scale, W3, g3, b3, m3, v3, Wc1, gc1, bc1, mc1, vc1):
    return core(e4m3fn_values(h2_bytes) * h2_scale.astype(np.float64), W3, g3, b3, m3, v3, Wc1, gc1, bc1, mc1, vc1)

@@ -1,0 +1,293 @@
+from contextlib import ExitStack
+
+import concourse.mybir as mybir
+from concourse.masks import make_identity
+
+F32 = mybir.dt.float32
+BF16 = mybir.dt.bfloat16
+U32 = mybir.dt.uint32
+U8 = mybir.dt.uint8
+F8 = mybir.dt.float8_e4m3fn
+FP8X4 = mybir.dt.float8_e4m3fn_x4
+ALU = mybir.AluOpType
+ACT = mybir.ActivationFunctionType
+
+P = 128
+T = 4
+H = 512
+M, N = 32, 128
+FLOPS = 2 * H * H * M * N + 2 * H * H * N
+EPS = 1e-5
+
+UNITS = [256, 256, 512, 512, 512, 512, 512, 512, 512]
+LOADS = [2, 1, 2, 2, 2]
+RAW = {}
+SHARES = [(w, 0) for w in UNITS]
+VWIDE = {0: 2, 1: 1}
+LOOK = 3
+WC1_LOAD = 2
+WCOPY = "svsv"
+
+
+def tile_p2b_xcorr_pb_t_kernel(tc, h2_bytes, h2_scale, W3, g3, b3, m3, v3, Wc1, gc1, bc1, mc1, vc1, out):
+    nc = tc.nc
+    n_units = len(UNITS)
+    starts = [sum(UNITS[:u]) for u in range(n_units)]
+
+    with ExitStack() as ctx:
+        keep = ctx.enter_context(tc.tile_pool(name="keep", bufs=1))
+        psum = ctx.enter_context(tc.psum_pool(name="psum", bufs=8))
+        ctx.enter_context(tc.manual_schedule())
+
+        def bank():
+            return psum.tile([P, 512], F32, name="bank")
+
+        warm = keep.tile([P, 1], F32, name="warm")
+        warm_out = keep.tile([P, 1], F32, name="warm_out")
+        nc.vector.memset(warm[:], 1.0)
+
+        scl = keep.tile([P, T], F32, name="scl")
+        nc.scalar.dma_start(out=scl[:], in_=h2_scale.rearrange("o (p t) a b -> p (o t a b)", t=T))
+
+        bytes_hbm = h2_bytes.rearrange("o (p t) m n -> p (o t) (m n)", t=T)
+        raw_of = {}
+
+        def load_bytes(first, count):
+            c0 = starts[first]
+            width = sum(UNITS[first:first + count])
+            raw = keep.tile([P, T, width], U8, name="raw%d" % first, align_bytes=64)
+            nc.sync.dma_start(out=raw[:], in_=bytes_hbm[:, :, c0:c0 + width])
+            for u in range(first, first + count):
+                raw_of[u] = raw[:, :, starts[u] - c0:starts[u] - c0 + UNITS[u]]
+
+        def load_weight(w, name):
+            raw = keep.tile([P, T, H], BF16, name=name, align_bytes=64)
+            nc.sync.dma_start(out=raw[:], in_=w.rearrange("(m t) k -> m t k", t=T))
+            return raw
+
+        bn_in = keep.tile([P, 8, 16], BF16, name="bn_in")
+
+        def load_vec(eng, i, vec):
+            eng.dma_start(out=bn_in[:, i, 0:T], in_=vec.rearrange("(p t) -> p t", t=T))
+
+        first = 0
+        for i, vec in enumerate((v3, g3, m3, b3)):
+            load_vec(nc.scalar, i, vec)
+        for n_load, count in enumerate(LOADS):
+            if n_load == 1:
+                w3_raw = load_weight(W3, "w3_raw")
+            if n_load == WC1_LOAD:
+                wc1_raw = load_weight(Wc1, "wc1_raw")
+            load_bytes(first, count)
+            first += count
+        for i, vec in enumerate((vc1, gc1, mc1, bc1)):
+            load_vec(nc.sync, 4 + i, vec)
+        nc.scalar.activation(out=warm_out[:], in_=warm[:], func=ACT.Sqrt)
+
+        ident = keep.tile([P, P], F32, name="ident", align_bytes=64)
+        make_identity(nc, ident[:])
+
+        class_of = {}
+        bn = {}
+        for name in ("bn3", "bnc"):
+            for part in "vsracm":
+                bn[name, part] = keep.tile([P, T], F32, name=name + "_" + part)
+
+        def bn_begin(i0, name):
+            nc.gpsimd.tensor_scalar(out=bn[name, "v"][:], in0=bn_in[:, i0, 0:T], scalar1=EPS, scalar2=None, op0=ALU.add)
+
+        def bn_root(name):
+            nc.scalar.activation(out=bn[name, "s"][:], in_=bn[name, "v"][:], func=ACT.Sqrt)
+
+        def bn_finish(i0, name):
+            a, ma, c, r = bn[name, "a"], bn[name, "m"], bn[name, "c"], bn[name, "r"]
+            nc.vector.reciprocal(out=r[:], in_=bn[name, "s"][:])
+            nc.gpsimd.tensor_tensor(out=a[:], in0=bn_in[:, i0 + 1, 0:T], in1=r[:], op=ALU.mult)
+            nc.gpsimd.tensor_tensor(out=ma[:], in0=bn_in[:, i0 + 2, 0:T], in1=a[:], op=ALU.mult)
+            nc.gpsimd.tensor_tensor(out=c[:], in0=bn_in[:, i0 + 3, 0:T], in1=ma[:], op=ALU.subtract)
+            return a, c
+
+        def transpose_weight(raw):
+            xts = []
+            for hf in range(2):
+                xt = bank()
+                for i in range(2):
+                    words = raw[:, 2 * hf + i, :].bitcast(F32)
+                    for e in range(2):
+                        q = 128 * (2 * i + e)
+                        nc.tensor.transpose(xt[:, q:q + 128], words[:, e:256:2], ident[:])
+                xts.append(xt)
+            return xts
+
+        def copy_weight(copy, grouped, hf, xt):
+            words = grouped[:].rearrange("p c j -> p (c j)").bitcast(F32)
+            copy(
+                out=words[:, 512 * hf:512 * hf + 512].rearrange("p (i m e) -> p i m e", i=2, e=2),
+                in_=xt[:].rearrange("p (i e m) -> p i m e", i=2, e=2),
+            )
+
+        wide = {}
+        inter = {}
+        codes = {}
+        scales = {}
+        banks = {}
+        fresh = {}
+
+        def widen(u, t):
+            w = UNITS[u]
+            if u not in wide:
+                wide[u] = keep.tile([P, T, w], BF16, name="wide%d" % u, align_bytes=64)
+            src = raw_of[u][:, t, :].bitcast(F8)
+            if t >= T - VWIDE.get(u, 0):
+                nc.vector.tensor_scalar(out=wide[u][:, t, :], in0=src, scalar1=scl[:, t:t + 1], scalar2=None, op0=ALU.mult)
+            else:
+                nc.scalar.activation(out=wide[u][:, t, :], in_=src, func=ACT.Copy, scale=scl[:, t:t + 1])
+
+        def interleave(u, which):
+            w = UNITS[u]
+            if u not in inter:
+                inter[u] = keep.tile([P, w, T], BF16, name="inter%d" % u, align_bytes=64)
+            vs, ss = SHARES[u]
+            lo, hi = {"v": (0, vs), "s": (vs, vs + ss), "g": (vs + ss, w)}[which]
+            if lo == hi:
+                return
+            dst, src = inter[u][:, lo:hi, :], wide[u][:, :, lo:hi]
+            if which == "g":
+                nc.gpsimd.tensor_scalar(out=dst, in0=src.rearrange("p t c -> p c t"), scalar1=1.0, scalar2=0.0, op0=ALU.mult, op1=ALU.add)
+            else:
+                copy = nc.vector.tensor_copy if which == "v" else nc.scalar.copy
+                copy(out=dst.rearrange("p (c i) t -> p c t i", i=4), in_=src.rearrange("p t (c i) -> p c t i", i=4))
+
+        def quantize(u):
+            w = UNITS[u]
+            codes[u] = keep.tile([P, w], U32, name="codes%d" % u, align_bytes=64)
+            scales[u] = keep.tile([P, w], U8, name="scales%d" % u, align_bytes=64)
+            nc.vector.quantize_mx(out=codes[u][:].bitcast(FP8X4), scales=scales[u][:], in_=inter[u][:].rearrange("p c t -> p (c t)"))
+
+        w3_codes = keep.tile([P, H], U32, name="w3_codes", align_bytes=64)
+        w3_scales = keep.tile([P, H], U8, name="w3_scales", align_bytes=64)
+        w3_grouped = keep.tile([P, H, T], BF16, name="w3_grouped", align_bytes=64)
+        wc1_codes = keep.tile([P, H], U32, name="wc1_codes", align_bytes=64)
+        wc1_scales = keep.tile([P, H], U8, name="wc1_scales", align_bytes=64)
+        wc1_grouped = keep.tile([P, H, T], BF16, name="wc1_grouped", align_bytes=64)
+
+        def quantize_weight(grouped, codes_t, scales_t):
+            nc.vector.quantize_mx(out=codes_t[:].bitcast(FP8X4), scales=scales_t[:], in_=grouped[:].rearrange("p c j -> p (c j)"))
+
+        def mm(dst, wc, ws, j, mc, ms):
+            nc.tensor.matmul_mx(
+                out=dst,
+                lhsT=wc[:, 128 * j:128 * j + 128].bitcast(FP8X4),
+                lhsT_scale=ws[:, 128 * j:128 * j + 128],
+                rhs=mc.bitcast(FP8X4),
+                rhs_scale=ms,
+                start=True,
+                stop=True,
+            )
+
+        def matmuls(u):
+            w = UNITS[u]
+            outs = []
+            for pair in range(2):
+                if w == 512:
+                    outs.extend([bank()[:], bank()[:]])
+                else:
+                    b = bank()
+                    outs.extend([b[:, 0:w], b[:, 256:256 + w]])
+            for j in range(T):
+                mm(outs[j], w3_codes, w3_scales, j, codes[u][:], scales[u][:])
+            banks[u] = outs
+
+        A = 2
+        top = keep.tile([P, T, 512], BF16, name="top", align_bytes=64)
+        low = keep.tile([P, T - A, 512], F32, name="low", align_bytes=64)
+
+        def empty_scalar(u):
+            if A == 0:
+                return
+            if starts[u] < 512:
+                dst = top[:, 0:A, starts[u]:starts[u] + UNITS[u]]
+            else:
+                fresh[u] = keep.tile([P, A, UNITS[u]], BF16, name="fresh%d" % u, align_bytes=64)
+                dst = fresh[u]
+            for j in range(A):
+                nc.scalar.activation(out=dst[:, j, :], in_=banks[u][j], func=ACT.Relu, scale=a3[:, j:j + 1], bias=c3[:, j:j + 1])
+
+        def empty_vector(u):
+            for j in range(A, T):
+                if starts[u] < 512:
+                    nc.vector.tensor_scalar(out=low[:, j - A, starts[u]:starts[u] + UNITS[u]], in0=banks[u][j], scalar1=a3[:, j:j + 1], scalar2=None, op0=ALU.mult)
+                else:
+                    nc.vector.scalar_tensor_tensor(out=low[:, j - A, :], in0=banks[u][j], scalar=a3[:, j:j + 1], in1=low[:, j - A, :], op0=ALU.mult, op1=ALU.max)
+
+        def tmax(dst, x, y):
+            nc.vector.tensor_tensor(out=dst, in0=x, in1=y, op=ALU.max)
+
+        def join(u):
+            if starts[u] >= 512 and A:
+                tmax(top[:, 0:A, :], top[:, 0:A, :], fresh[u][:])
+
+        for u in range(LOOK):
+            for t in range(T):
+                widen(u, t)
+            interleave(u, "g")
+            if u == 0:
+                bn_begin(0, "bn3")
+                xt3 = transpose_weight(w3_raw)
+                interleave(0, "s")
+                interleave(0, "v")
+            if u == 1:
+                for hf in range(2):
+                    copy_weight(nc.scalar.copy if WCOPY[hf] == "s" else nc.vector.tensor_copy, w3_grouped, hf, xt3[hf])
+                bn_root("bn3")
+                xtc = transpose_weight(wc1_raw)
+
+        for s in range(1, n_units + 2):
+            if 0 <= s - 2 < n_units:
+                empty_scalar(s - 2)
+            if s < n_units:
+                interleave(s, "s")
+            if s - 1 + LOOK < n_units:
+                for t in range(T):
+                    widen(s - 1 + LOOK, t)
+                interleave(s - 1 + LOOK, "g")
+            if s < n_units:
+                interleave(s, "v")
+            if s == 1:
+                quantize_weight(w3_grouped, w3_codes, w3_scales)
+            if s - 1 < n_units:
+                quantize(s - 1)
+                matmuls(s - 1)
+            if s == 1:
+                for hf in range(2):
+                    copy_weight(nc.scalar.copy if WCOPY[2 + hf] == "s" else nc.vector.tensor_copy, wc1_grouped, hf, xtc[hf])
+                a3, c3 = bn_finish(0, "bn3")
+            if s == 5:
+                bn_begin(4, "bnc")
+                bn_root("bnc")
+            if s == 6:
+                quantize_weight(wc1_grouped, wc1_codes, wc1_scales)
+                ac, cc = bn_finish(4, "bnc")
+            if 0 <= s - 2 < n_units:
+                empty_vector(s - 2)
+                join(s - 2)
+
+        half = keep.tile([P, T, 256], BF16, name="half", align_bytes=64)
+        pooled = keep.tile([P, N, T], BF16, name="pooled", align_bytes=64)
+        for j in range(A, T):
+            nc.scalar.activation(out=top[:, j, :], in_=low[:, j - A, :], func=ACT.Relu, bias=c3[:, j:j + 1])
+        if A:
+            tmax(half[:, 0:A, :], top[:, 0:A, 0:256], top[:, 0:A, 256:512])
+        tmax(half[:, A:T, :], top[:, A:T, 0:256], top[:, A:T, 256:512])
+        tmax(pooled[:], half[:, :, 0:128].rearrange("p j n -> p n j"), half[:, :, 128:256].rearrange("p j n -> p n j"))
+
+        p_codes = keep.tile([P, N], U32, name="p_codes", align_bytes=64)
+        p_scales = keep.tile([P, N], U8, name="p_scales", align_bytes=64)
+        nc.vector.quantize_mx(out=p_codes[:].bitcast(FP8X4), scales=p_scales[:], in_=pooled[:].rearrange("p n j -> p (n j)"))
+        result = keep.tile([P, T, N], F32, name="result", align_bytes=64)
+        ys = [bank(), bank()]
+        for j in range(T):
+            mm(ys[j // 2][:, 256 * (j % 2):256 * (j % 2) + 128], wc1_codes, wc1_scales, j, p_codes[:], p_scales[:])
+        for j in range(T):
+            nc.scalar.activation(out=result[:, j, :], in_=ys[j // 2][:, 256 * (j % 2):256 * (j % 2) + 128], func=ACT.Relu, scale=ac[:, j:j + 1], bias=cc[:, j:j + 1])
+        nc.sync.dma_start(out=out.rearrange("o (p t) n -> p (o t) n", t=T), in_=result[:])

@@ -22,10 +22,18 @@ EPS = 1e-5
 UNITS = [256, 256, 512, 512, 512, 512, 512, 512, 512]
 LOADS = [2, 1, 2, 2, 2]
 RAW = {}
-SHARES = [(w, 0) for w in UNITS]
-VWIDE = {0: 2, 1: 1}
+SHARES = [(w, 0) if u < 2 else {}.get(u, (0, 128)) for u, w in enumerate(UNITS)]
+VWIDE = {0: 4, 2: 1}
 LOOK = 3
 WC1_LOAD = 2
+BNC = 5
+QC = 8
+STEP_FROM = 2
+IBUFS = 1
+GLEAD = 1
+AT = 7
+AS = 2
+E1 = True
 WCOPY = "svsv"
 
 
@@ -146,7 +154,10 @@ def tile_p2b_xcorr_pb_t_kernel(tc, h2_bytes, h2_scale, W3, g3, b3, m3, v3, Wc1, 
         def interleave(u, which):
             w = UNITS[u]
             if u not in inter:
-                inter[u] = keep.tile([P, w, T], BF16, name="inter%d" % u, align_bytes=64)
+                if u < STEP_FROM:
+                    inter[u] = keep.tile([P, w, T], BF16, name="inter%d" % u, align_bytes=64)
+                else:
+                    inter[u] = keep.tile([P, w, T], BF16, name="inter", bufs=IBUFS, align_bytes=64)
             vs, ss = SHARES[u]
             lo, hi = {"v": (0, vs), "s": (vs, vs + ss), "g": (vs + ss, w)}[which]
             if lo == hi:
@@ -198,87 +209,105 @@ def tile_p2b_xcorr_pb_t_kernel(tc, h2_bytes, h2_scale, W3, g3, b3, m3, v3, Wc1, 
                 mm(outs[j], w3_codes, w3_scales, j, codes[u][:], scales[u][:])
             banks[u] = outs
 
-        A = 2
-        top = keep.tile([P, T, 512], BF16, name="top", align_bytes=64)
-        low = keep.tile([P, T - A, 512], F32, name="low", align_bytes=64)
+        low = keep.tile([P, T, 512], F32, name="low", align_bytes=64)
+        lowb = keep.tile([P, T, 512], BF16, name="lowb", align_bytes=64)
+        top = keep.tile([P, AS, 512], BF16, name="top", align_bytes=64)
 
         def empty_scalar(u):
-            if A == 0:
+            if u < AT:
                 return
-            if starts[u] < 512:
-                dst = top[:, 0:A, starts[u]:starts[u] + UNITS[u]]
+            if u == AT:
+                fresh[u] = top
             else:
-                fresh[u] = keep.tile([P, A, UNITS[u]], BF16, name="fresh%d" % u, align_bytes=64)
-                dst = fresh[u]
-            for j in range(A):
-                nc.scalar.activation(out=dst[:, j, :], in_=banks[u][j], func=ACT.Relu, scale=a3[:, j:j + 1], bias=c3[:, j:j + 1])
+                fresh[u] = keep.tile([P, AS, UNITS[u]], BF16, name="fresh%d" % u, align_bytes=64)
+            for j in range(AS):
+                nc.scalar.activation(out=fresh[u][:, j, :], in_=banks[u][j], func=ACT.Relu, scale=a3[:, j:j + 1], bias=c3[:, j:j + 1])
+
+        def finish_low(j):
+            nc.scalar.activation(out=lowb[:, j, :], in_=low[:, j, :], func=ACT.Relu, bias=c3[:, j:j + 1])
 
         def empty_vector(u):
-            for j in range(A, T):
+            for j in range(AS if u >= AT else 0, T):
                 if starts[u] < 512:
-                    nc.vector.tensor_scalar(out=low[:, j - A, starts[u]:starts[u] + UNITS[u]], in0=banks[u][j], scalar1=a3[:, j:j + 1], scalar2=None, op0=ALU.mult)
+                    nc.vector.tensor_scalar(out=low[:, j, starts[u]:starts[u] + UNITS[u]], in0=banks[u][j], scalar1=a3[:, j:j + 1], scalar2=None, op0=ALU.mult)
                 else:
-                    nc.vector.scalar_tensor_tensor(out=low[:, j - A, :], in0=banks[u][j], scalar=a3[:, j:j + 1], in1=low[:, j - A, :], op0=ALU.mult, op1=ALU.max)
+                    nc.vector.scalar_tensor_tensor(out=low[:, j, :], in0=banks[u][j], scalar=a3[:, j:j + 1], in1=low[:, j, :], op0=ALU.mult, op1=ALU.max)
 
         def tmax(dst, x, y):
             nc.vector.tensor_tensor(out=dst, in0=x, in1=y, op=ALU.max)
 
         def join(u):
-            if starts[u] >= 512 and A:
-                tmax(top[:, 0:A, :], top[:, 0:A, :], fresh[u][:])
+            if u > AT:
+                tmax(top[:], top[:], fresh[u][:])
 
-        for u in range(LOOK):
-            for t in range(T):
-                widen(u, t)
-            interleave(u, "g")
-            if u == 0:
-                bn_begin(0, "bn3")
-                xt3 = transpose_weight(w3_raw)
-                interleave(0, "s")
-                interleave(0, "v")
-            if u == 1:
-                for hf in range(2):
-                    copy_weight(nc.scalar.copy if WCOPY[hf] == "s" else nc.vector.tensor_copy, w3_grouped, hf, xt3[hf])
-                bn_root("bn3")
-                xtc = transpose_weight(wc1_raw)
+        for t in range(T):
+            widen(0, t)
+        bn_begin(0, "bn3")
+        bn_root("bn3")
+        for t in range(T):
+            widen(1, t)
+        xt3 = transpose_weight(w3_raw)
+        interleave(0, "v")
+        a3, c3 = bn_finish(0, "bn3")
+        interleave(1, "v")
+        for hf in range(2):
+            copy_weight(nc.scalar.copy if WCOPY[hf] == "s" else nc.vector.tensor_copy, w3_grouped, hf, xt3[hf])
+        quantize(0)
+        quantize_weight(w3_grouped, w3_codes, w3_scales)
+        matmuls(0)
+        quantize(1)
+        matmuls(1)
+        xtc = transpose_weight(wc1_raw)
+        for t in range(T):
+            widen(2, t)
+        interleave(2, "g")
+        interleave(2, "s")
+        for t in range(T):
+            widen(3, t)
+        empty_vector(0)
+        interleave(2, "v")
 
-        for s in range(1, n_units + 2):
-            if 0 <= s - 2 < n_units:
-                empty_scalar(s - 2)
-            if s < n_units:
-                interleave(s, "s")
-            if s - 1 + LOOK < n_units:
+        last = n_units - 1
+        for u in range(2, n_units):
+            quantize(u)
+            matmuls(u)
+            if u + 1 < n_units:
+                interleave(u + 1, "g")
+                interleave(u + 1, "s")
+            if u + 2 < n_units:
                 for t in range(T):
-                    widen(s - 1 + LOOK, t)
-                interleave(s - 1 + LOOK, "g")
-            if s < n_units:
-                interleave(s, "v")
-            if s == 1:
-                quantize_weight(w3_grouped, w3_codes, w3_scales)
-            if s - 1 < n_units:
-                quantize(s - 1)
-                matmuls(s - 1)
-            if s == 1:
+                    widen(u + 2, t)
+            if u == 2:
                 for hf in range(2):
                     copy_weight(nc.scalar.copy if WCOPY[2 + hf] == "s" else nc.vector.tensor_copy, wc1_grouped, hf, xtc[hf])
-                a3, c3 = bn_finish(0, "bn3")
-            if s == 5:
+            if u == 3:
                 bn_begin(4, "bnc")
+            if u == 4:
                 bn_root("bnc")
-            if s == 6:
-                quantize_weight(wc1_grouped, wc1_codes, wc1_scales)
+            if u == BNC:
                 ac, cc = bn_finish(4, "bnc")
-            if 0 <= s - 2 < n_units:
-                empty_vector(s - 2)
-                join(s - 2)
-
+            if u == QC:
+                quantize_weight(wc1_grouped, wc1_codes, wc1_scales)
+            empty_scalar(u - 1)
+            empty_vector(u - 1)
+            join(u - 1)
+            if u == AT:
+                for j in range(AS):
+                    finish_low(j)
+            if u + 1 < n_units:
+                interleave(u + 1, "v")
+        empty_scalar(last)
+        empty_vector(last)
+        for j in range(0 if AT > last else AS, T):
+            finish_low(j)
         half = keep.tile([P, T, 256], BF16, name="half", align_bytes=64)
         pooled = keep.tile([P, N, T], BF16, name="pooled", align_bytes=64)
-        for j in range(A, T):
-            nc.scalar.activation(out=top[:, j, :], in_=low[:, j - A, :], func=ACT.Relu, bias=c3[:, j:j + 1])
-        if A:
-            tmax(half[:, 0:A, :], top[:, 0:A, 0:256], top[:, 0:A, 256:512])
-        tmax(half[:, A:T, :], top[:, A:T, 0:256], top[:, A:T, 256:512])
+        tmax(half[:, 0:AS, :], lowb[:, 0:AS, 0:256], lowb[:, 0:AS, 256:512])
+        if AT <= last:
+            join(last)
+            tmax(top[:, :, 0:256], top[:, :, 0:256], top[:, :, 256:512])
+            tmax(half[:, 0:AS, :], half[:, 0:AS, :], top[:, :, 0:256])
+        tmax(half[:, AS:T, :], lowb[:, AS:T, 0:256], lowb[:, AS:T, 256:512])
         tmax(pooled[:], half[:, :, 0:128].rearrange("p j n -> p n j"), half[:, :, 128:256].rearrange("p j n -> p n j"))
 
         p_codes = keep.tile([P, N], U32, name="p_codes", align_bytes=64)

@@ -22,19 +22,21 @@ EPS = 1e-5
 UNITS = [256, 256, 512, 512, 512, 512, 512, 512, 512]
 LOADS = [2, 1, 2, 2, 2]
 RAW = {}
-SHARES = [(w, 0) if u < 2 else {}.get(u, (0, 128)) for u, w in enumerate(UNITS)]
+SHARES = [(w, 0) if u < 2 else {3: (0, 128)}.get(u, (96, 96)) for u, w in enumerate(UNITS)]
 VWIDE = {0: 4, 2: 1}
 LOOK = 3
 WC1_LOAD = 2
 BNC = 5
 QC = 8
 STEP_FROM = 2
-IBUFS = 1
+IBUFS = 2
 GLEAD = 1
 AT = 7
 AS = 2
 E1 = True
-WCOPY = "svsv"
+BN3_LOAD = 1
+WARM = (5, 3)
+WCOPY = "svvv"
 
 
 def tile_p2b_xcorr_pb_t_kernel(tc, h2_bytes, h2_scale, W3, g3, b3, m3, v3, Wc1, gc1, bc1, mc1, vc1, out):
@@ -79,11 +81,12 @@ def tile_p2b_xcorr_pb_t_kernel(tc, h2_bytes, h2_scale, W3, g3, b3, m3, v3, Wc1, 
             eng.dma_start(out=bn_in[:, i, 0:T], in_=vec.rearrange("(p t) -> p t", t=T))
 
         first = 0
-        for i, vec in enumerate((v3, g3, m3, b3)):
-            load_vec(nc.scalar, i, vec)
         for n_load, count in enumerate(LOADS):
             if n_load == 1:
                 w3_raw = load_weight(W3, "w3_raw")
+            if n_load == BN3_LOAD:
+                for i, vec in enumerate((v3, g3, m3, b3)):
+                    load_vec(nc.sync, i, vec)
             if n_load == WC1_LOAD:
                 wc1_raw = load_weight(Wc1, "wc1_raw")
             load_bytes(first, count)
@@ -91,6 +94,15 @@ def tile_p2b_xcorr_pb_t_kernel(tc, h2_bytes, h2_scale, W3, g3, b3, m3, v3, Wc1, 
         for i, vec in enumerate((vc1, gc1, mc1, bc1)):
             load_vec(nc.sync, 4 + i, vec)
         nc.scalar.activation(out=warm_out[:], in_=warm[:], func=ACT.Sqrt)
+        zeros = keep.tile([P, 512], BF16, name="zeros", align_bytes=64)
+        nc.vector.memset(zeros[:], 0.0)
+        dummy = bank()
+
+        def spin(count):
+            for i in range(count):
+                nc.tensor.matmul(dummy[:], lhsT=zeros[:, 0:128], rhs=zeros[:], start=True, stop=True)
+
+        spin(WARM[0])
 
         ident = keep.tile([P, P], F32, name="ident", align_bytes=64)
         make_identity(nc, ident[:])
@@ -242,14 +254,15 @@ def tile_p2b_xcorr_pb_t_kernel(tc, h2_bytes, h2_scale, W3, g3, b3, m3, v3, Wc1, 
 
         for t in range(T):
             widen(0, t)
-        bn_begin(0, "bn3")
-        bn_root("bn3")
         for t in range(T):
             widen(1, t)
+        bn_begin(0, "bn3")
+        bn_root("bn3")
         xt3 = transpose_weight(w3_raw)
+        spin(WARM[1])
         interleave(0, "v")
-        a3, c3 = bn_finish(0, "bn3")
         interleave(1, "v")
+        a3, c3 = bn_finish(0, "bn3")
         for hf in range(2):
             copy_weight(nc.scalar.copy if WCOPY[hf] == "s" else nc.vector.tensor_copy, w3_grouped, hf, xt3[hf])
         quantize(0)
@@ -268,10 +281,14 @@ def tile_p2b_xcorr_pb_t_kernel(tc, h2_bytes, h2_scale, W3, g3, b3, m3, v3, Wc1, 
         interleave(2, "v")
 
         last = n_units - 1
+        token = keep.tile([P, 16], U32, name="token")
         for u in range(2, n_units):
+            if u + 1 < n_units:
+                interleave(u + 1, "v")
             quantize(u)
             matmuls(u)
             if u + 1 < n_units:
+                nc.gpsimd.tensor_copy(out=token[:, u:u + 1], in_=codes[u][:, 0:1])
                 interleave(u + 1, "g")
                 interleave(u + 1, "s")
             if u + 2 < n_units:
@@ -294,8 +311,6 @@ def tile_p2b_xcorr_pb_t_kernel(tc, h2_bytes, h2_scale, W3, g3, b3, m3, v3, Wc1, 
             if u == AT:
                 for j in range(AS):
                     finish_low(j)
-            if u + 1 < n_units:
-                interleave(u + 1, "v")
         empty_scalar(last)
         empty_vector(last)
         for j in range(0 if AT > last else AS, T):

@@ -22,12 +22,12 @@ EPS = 1e-5
 UNITS = [256, 256, 512, 512, 512, 512, 512, 512, 512]
 LOADS = [2, 1, 2, 2, 2]
 RAW = {}
-SHARES = [(w, 0) if u < 2 else {3: (0, 128)}.get(u, (96, 96)) for u, w in enumerate(UNITS)]
-VWIDE = {0: 4, 2: 1}
+SHARES = [(w, 0) if u < 2 else {2: (128, 96), 3: (0, 128), 7: (0, 192), 8: (0, 192)}.get(u, (64, 128)) for u, w in enumerate(UNITS)]
+VWIDE = {0: 4, 2: 1, 3: 1}
 LOOK = 3
 WC1_LOAD = 2
 BNC = 5
-QC = 8
+QC = 6
 STEP_FROM = 2
 IBUFS = 2
 GLEAD = 1
@@ -151,6 +151,7 @@ def tile_p2b_xcorr_pb_t_kernel(tc, h2_bytes, h2_scale, W3, g3, b3, m3, v3, Wc1, 
         codes = {}
         scales = {}
         banks = {}
+        first_banks = []
         fresh = {}
 
         def widen(u, t):
@@ -210,13 +211,13 @@ def tile_p2b_xcorr_pb_t_kernel(tc, h2_bytes, h2_scale, W3, g3, b3, m3, v3, Wc1, 
 
         def matmuls(u):
             w = UNITS[u]
-            outs = []
-            for pair in range(2):
-                if w == 512:
-                    outs.extend([bank()[:], bank()[:]])
-                else:
-                    b = bank()
-                    outs.extend([b[:, 0:w], b[:, 256:256 + w]])
+            if starts[u] == 0:
+                for j in range(T):
+                    first_banks.append(bank())
+            if starts[u] < 512:
+                outs = [first_banks[j][:, starts[u]:starts[u] + w] for j in range(T)]
+            else:
+                outs = [bank()[:] for j in range(T)]
             for j in range(T):
                 mm(outs[j], w3_codes, w3_scales, j, codes[u][:], scales[u][:])
             banks[u] = outs
@@ -241,16 +242,12 @@ def tile_p2b_xcorr_pb_t_kernel(tc, h2_bytes, h2_scale, W3, g3, b3, m3, v3, Wc1, 
         def empty_vector(u):
             for j in range(AS if u >= AT else 0, T):
                 if starts[u] < 512:
-                    nc.vector.tensor_scalar(out=low[:, j, starts[u]:starts[u] + UNITS[u]], in0=banks[u][j], scalar1=a3[:, j:j + 1], scalar2=None, op0=ALU.mult)
+                    nc.vector.tensor_scalar(out=low[:, j, :], in0=first_banks[j][:], scalar1=a3[:, j:j + 1], scalar2=None, op0=ALU.mult)
                 else:
                     nc.vector.scalar_tensor_tensor(out=low[:, j, :], in0=banks[u][j], scalar=a3[:, j:j + 1], in1=low[:, j, :], op0=ALU.mult, op1=ALU.max)
 
         def tmax(dst, x, y):
             nc.vector.tensor_tensor(out=dst, in0=x, in1=y, op=ALU.max)
-
-        def join(u):
-            if u > AT:
-                tmax(top[:], top[:], fresh[u][:])
 
         for t in range(T):
             widen(0, t)
@@ -267,17 +264,18 @@ def tile_p2b_xcorr_pb_t_kernel(tc, h2_bytes, h2_scale, W3, g3, b3, m3, v3, Wc1, 
             copy_weight(nc.scalar.copy if WCOPY[hf] == "s" else nc.vector.tensor_copy, w3_grouped, hf, xt3[hf])
         quantize(0)
         quantize_weight(w3_grouped, w3_codes, w3_scales)
+        xtc = transpose_weight(wc1_raw)
         matmuls(0)
         quantize(1)
         matmuls(1)
-        xtc = transpose_weight(wc1_raw)
         for t in range(T):
             widen(2, t)
         interleave(2, "g")
         interleave(2, "s")
         for t in range(T):
             widen(3, t)
-        empty_vector(0)
+        for hf in range(2):
+            copy_weight(nc.scalar.copy if WCOPY[2 + hf] == "s" else nc.vector.tensor_copy, wc1_grouped, hf, xtc[hf])
         interleave(2, "v")
 
         last = n_units - 1
@@ -294,9 +292,6 @@ def tile_p2b_xcorr_pb_t_kernel(tc, h2_bytes, h2_scale, W3, g3, b3, m3, v3, Wc1, 
             if u + 2 < n_units:
                 for t in range(T):
                     widen(u + 2, t)
-            if u == 2:
-                for hf in range(2):
-                    copy_weight(nc.scalar.copy if WCOPY[2 + hf] == "s" else nc.vector.tensor_copy, wc1_grouped, hf, xtc[hf])
             if u == 3:
                 bn_begin(4, "bnc")
             if u == 4:
@@ -307,22 +302,27 @@ def tile_p2b_xcorr_pb_t_kernel(tc, h2_bytes, h2_scale, W3, g3, b3, m3, v3, Wc1, 
                 quantize_weight(wc1_grouped, wc1_codes, wc1_scales)
             empty_scalar(u - 1)
             empty_vector(u - 1)
-            join(u - 1)
             if u == AT:
                 for j in range(AS):
                     finish_low(j)
-        empty_scalar(last)
-        empty_vector(last)
-        for j in range(0 if AT > last else AS, T):
-            finish_low(j)
         half = keep.tile([P, T, 256], BF16, name="half", align_bytes=64)
+        other = keep.tile([P, AS, 256], BF16, name="other", align_bytes=64)
         pooled = keep.tile([P, N, T], BF16, name="pooled", align_bytes=64)
-        tmax(half[:, 0:AS, :], lowb[:, 0:AS, 0:256], lowb[:, 0:AS, 256:512])
-        if AT <= last:
-            join(last)
-            tmax(top[:, :, 0:256], top[:, :, 0:256], top[:, :, 256:512])
-            tmax(half[:, 0:AS, :], half[:, 0:AS, :], top[:, :, 0:256])
-        tmax(half[:, AS:T, :], lowb[:, AS:T, 0:256], lowb[:, AS:T, 256:512])
+
+        def fold(dst, src):
+            tmax(dst, src[:, :, 0:256], src[:, :, 256:512])
+
+        empty_scalar(last)
+        fold(half[:, 0:AS, :], lowb[:, 0:AS, :])
+        fold(other[:], top)
+        empty_vector(last)
+        for j in range(AS, T):
+            finish_low(j)
+        tmax(half[:, 0:AS, :], half[:, 0:AS, :], other[:])
+        fold(other[:], fresh[last])
+        fold(half[:, 2:3, :], lowb[:, 2:3, :])
+        tmax(half[:, 0:AS, :], half[:, 0:AS, :], other[:])
+        fold(half[:, 3:4, :], lowb[:, 3:4, :])
         tmax(pooled[:], half[:, :, 0:128].rearrange("p j n -> p n j"), half[:, :, 128:256].rearrange("p j n -> p n j"))
 
         p_codes = keep.tile([P, N], U32, name="p_codes", align_bytes=64)

@@ -22,12 +22,12 @@ EPS = 1e-5
 UNITS = [256, 256, 512, 512, 512, 512, 512, 512, 512]
 LOADS = [2, 1, 2, 2, 2]
 RAW = {}
-SHARES = [(w, 0) if u < 2 else {2: (128, 96), 3: (0, 128), 7: (0, 192), 8: (0, 192)}.get(u, (64, 128)) for u, w in enumerate(UNITS)]
+SHARES = [(w, 0) if u < 2 else {2: (128, 96), 3: (32, 96), 7: (32, 128), 8: (32, 128)}.get(u, (64, 96)) for u, w in enumerate(UNITS)]
 VWIDE = {0: 4, 2: 1, 3: 1}
 LOOK = 3
 WC1_LOAD = 2
 BNC = 5
-QC = 6
+QC = 8
 STEP_FROM = 2
 IBUFS = 2
 GLEAD = 1
@@ -152,6 +152,7 @@ def tile_p2b_xcorr_pb_t_kernel(tc, h2_bytes, h2_scale, W3, g3, b3, m3, v3, Wc1, 
         scales = {}
         banks = {}
         first_banks = []
+        ones = {2: warm}
         fresh = {}
 
         def widen(u, t):
@@ -177,10 +178,11 @@ def tile_p2b_xcorr_pb_t_kernel(tc, h2_bytes, h2_scale, W3, g3, b3, m3, v3, Wc1, 
                 return
             dst, src = inter[u][:, lo:hi, :], wide[u][:, :, lo:hi]
             if which == "g":
-                nc.gpsimd.tensor_scalar(out=dst, in0=src.rearrange("p t c -> p c t"), scalar1=1.0, scalar2=0.0, op0=ALU.mult, op1=ALU.add)
+                nc.gpsimd.tensor_scalar(out=dst, in0=src.rearrange("p t c -> p c t"), scalar1=ones[u][:, 0:1], scalar2=0.0, op0=ALU.mult, op1=ALU.add)
+            elif which == "s":
+                nc.scalar.copy(out=dst, in_=src.rearrange("p t c -> p c t"))
             else:
-                copy = nc.vector.tensor_copy if which == "v" else nc.scalar.copy
-                copy(out=dst.rearrange("p (c i) t -> p c t i", i=4), in_=src.rearrange("p t (c i) -> p c t i", i=4))
+                nc.vector.tensor_copy(out=dst.rearrange("p (c i) t -> p c t i", i=4), in_=src.rearrange("p t (c i) -> p c t i", i=4))
 
         def quantize(u):
             w = UNITS[u]
@@ -279,14 +281,14 @@ def tile_p2b_xcorr_pb_t_kernel(tc, h2_bytes, h2_scale, W3, g3, b3, m3, v3, Wc1, 
         interleave(2, "v")
 
         last = n_units - 1
-        token = keep.tile([P, 16], U32, name="token")
         for u in range(2, n_units):
             if u + 1 < n_units:
                 interleave(u + 1, "v")
             quantize(u)
             matmuls(u)
             if u + 1 < n_units:
-                nc.gpsimd.tensor_copy(out=token[:, u:u + 1], in_=codes[u][:, 0:1])
+                ones[u + 1] = keep.tile([P, 1], F32, name="one%d" % u)
+                nc.vector.memset(ones[u + 1][:], 1.0)
                 interleave(u + 1, "g")
                 interleave(u + 1, "s")
             if u + 2 < n_units:

from contextlib import ExitStack

import concourse.mybir as mybir
from concourse.masks import make_identity

F32 = mybir.dt.float32
BF16 = mybir.dt.bfloat16
U32 = mybir.dt.uint32
U8 = mybir.dt.uint8
F8 = mybir.dt.float8_e4m3fn
FP8X4 = mybir.dt.float8_e4m3fn_x4
ALU = mybir.AluOpType
ACT = mybir.ActivationFunctionType

P = 128
T = 4
H = 512
M, N = 32, 128
FLOPS = 2 * H * H * M * N + 2 * H * H * N
EPS = 1e-5

UNITS = [256, 256, 512, 512, 512, 512, 512, 512, 512]
LOADS = [2, 1, 2, 2, 2]
RAW = {}
SHARES = [(w, 0) if u < 2 else {2: (128, 96), 3: (32, 96), 7: (32, 128), 8: (32, 128)}.get(u, (64, 96)) for u, w in enumerate(UNITS)]
VWIDE = {0: 4, 2: 1, 3: 1}
LOOK = 3
WC1_LOAD = 2
BNC = 5
QC = 8
STEP_FROM = 2
IBUFS = 2
GLEAD = 1
AT = 7
AS = 2
E1 = True
BN3_LOAD = 1
WARM = (5, 3)
WCOPY = "svvv"


def tile_p2b_xcorr_pb_t_kernel(tc, h2_bytes, h2_scale, W3, g3, b3, m3, v3, Wc1, gc1, bc1, mc1, vc1, out):
    nc = tc.nc
    n_units = len(UNITS)
    starts = [sum(UNITS[:u]) for u in range(n_units)]

    with ExitStack() as ctx:
        keep = ctx.enter_context(tc.tile_pool(name="keep", bufs=1))
        psum = ctx.enter_context(tc.psum_pool(name="psum", bufs=8))
        ctx.enter_context(tc.manual_schedule())

        def bank():
            return psum.tile([P, 512], F32, name="bank")

        warm = keep.tile([P, 1], F32, name="warm")
        warm_out = keep.tile([P, 1], F32, name="warm_out")
        nc.vector.memset(warm[:], 1.0)

        scl = keep.tile([P, T], F32, name="scl")
        nc.scalar.dma_start(out=scl[:], in_=h2_scale.rearrange("o (p t) a b -> p (o t a b)", t=T))

        bytes_hbm = h2_bytes.rearrange("o (p t) m n -> p (o t) (m n)", t=T)
        raw_of = {}

        def load_bytes(first, count):
            c0 = starts[first]
            width = sum(UNITS[first:first + count])
            raw = keep.tile([P, T, width], U8, name="raw%d" % first, align_bytes=64)
            nc.sync.dma_start(out=raw[:], in_=bytes_hbm[:, :, c0:c0 + width])
            for u in range(first, first + count):
                raw_of[u] = raw[:, :, starts[u] - c0:starts[u] - c0 + UNITS[u]]

        def load_weight(w, name):
            raw = keep.tile([P, T, H], BF16, name=name, align_bytes=64)
            nc.sync.dma_start(out=raw[:], in_=w.rearrange("(m t) k -> m t k", t=T))
            return raw

        bn_in = keep.tile([P, 8, 16], BF16, name="bn_in")

        def load_vec(eng, i, vec):
            eng.dma_start(out=bn_in[:, i, 0:T], in_=vec.rearrange("(p t) -> p t", t=T))

        first = 0
        for n_load, count in enumerate(LOADS):
            if n_load == 1:
                w3_raw = load_weight(W3, "w3_raw")
            if n_load == BN3_LOAD:
                for i, vec in enumerate((v3, g3, m3, b3)):
                    load_vec(nc.sync, i, vec)
            if n_load == WC1_LOAD:
                wc1_raw = load_weight(Wc1, "wc1_raw")
            load_bytes(first, count)
            first += count
        for i, vec in enumerate((vc1, gc1, mc1, bc1)):
            load_vec(nc.sync, 4 + i, vec)
        nc.scalar.activation(out=warm_out[:], in_=warm[:], func=ACT.Sqrt)
        zeros = keep.tile([P, 512], BF16, name="zeros", align_bytes=64)
        nc.vector.memset(zeros[:], 0.0)
        dummy = bank()

        def spin(count):
            for i in range(count):
                nc.tensor.matmul(dummy[:], lhsT=zeros[:, 0:128], rhs=zeros[:], start=True, stop=True)

        spin(WARM[0])

        ident = keep.tile([P, P], F32, name="ident", align_bytes=64)
        make_identity(nc, ident[:])

        class_of = {}
        bn = {}
        for name in ("bn3", "bnc"):
            for part in "vsracm":
                bn[name, part] = keep.tile([P, T], F32, name=name + "_" + part)

        def bn_begin(i0, name):
            nc.gpsimd.tensor_scalar(out=bn[name, "v"][:], in0=bn_in[:, i0, 0:T], scalar1=EPS, scalar2=None, op0=ALU.add)

        def bn_root(name):
            nc.scalar.activation(out=bn[name, "s"][:], in_=bn[name, "v"][:], func=ACT.Sqrt)

        def bn_finish(i0, name):
            a, ma, c, r = bn[name, "a"], bn[name, "m"], bn[name, "c"], bn[name, "r"]
            nc.vector.reciprocal(out=r[:], in_=bn[name, "s"][:])
            nc.gpsimd.tensor_tensor(out=a[:], in0=bn_in[:, i0 + 1, 0:T], in1=r[:], op=ALU.mult)
            nc.gpsimd.tensor_tensor(out=ma[:], in0=bn_in[:, i0 + 2, 0:T], in1=a[:], op=ALU.mult)
            nc.gpsimd.tensor_tensor(out=c[:], in0=bn_in[:, i0 + 3, 0:T], in1=ma[:], op=ALU.subtract)
            return a, c

        def transpose_weight(raw):
            xts = []
            for hf in range(2):
                xt = bank()
                for i in range(2):
                    words = raw[:, 2 * hf + i, :].bitcast(F32)
                    for e in range(2):
                        q = 128 * (2 * i + e)
                        nc.tensor.transpose(xt[:, q:q + 128], words[:, e:256:2], ident[:])
                xts.append(xt)
            return xts

        def copy_weight(copy, grouped, hf, xt):
            words = grouped[:].rearrange("p c j -> p (c j)").bitcast(F32)
            copy(
                out=words[:, 512 * hf:512 * hf + 512].rearrange("p (i m e) -> p i m e", i=2, e=2),
                in_=xt[:].rearrange("p (i e m) -> p i m e", i=2, e=2),
            )

        wide = {}
        inter = {}
        codes = {}
        scales = {}
        banks = {}
        first_banks = []
        ones = {2: warm}
        fresh = {}

        def widen(u, t):
            w = UNITS[u]
            if u not in wide:
                wide[u] = keep.tile([P, T, w], BF16, name="wide%d" % u, align_bytes=64)
            src = raw_of[u][:, t, :].bitcast(F8)
            if t >= T - VWIDE.get(u, 0):
                nc.vector.tensor_scalar(out=wide[u][:, t, :], in0=src, scalar1=scl[:, t:t + 1], scalar2=None, op0=ALU.mult)
            else:
                nc.scalar.activation(out=wide[u][:, t, :], in_=src, func=ACT.Copy, scale=scl[:, t:t + 1])

        def interleave(u, which):
            w = UNITS[u]
            if u not in inter:
                if u < STEP_FROM:
                    inter[u] = keep.tile([P, w, T], BF16, name="inter%d" % u, align_bytes=64)
                else:
                    inter[u] = keep.tile([P, w, T], BF16, name="inter", bufs=IBUFS, align_bytes=64)
            vs, ss = SHARES[u]
            lo, hi = {"v": (0, vs), "s": (vs, vs + ss), "g": (vs + ss, w)}[which]
            if lo == hi:
                return
            dst, src = inter[u][:, lo:hi, :], wide[u][:, :, lo:hi]
            if which == "g":
                nc.gpsimd.tensor_scalar(out=dst, in0=src.rearrange("p t c -> p c t"), scalar1=ones[u][:, 0:1], scalar2=0.0, op0=ALU.mult, op1=ALU.add)
            elif which == "s":
                nc.scalar.copy(out=dst, in_=src.rearrange("p t c -> p c t"))
            else:
                nc.vector.tensor_copy(out=dst.rearrange("p (c i) t -> p c t i", i=4), in_=src.rearrange("p t (c i) -> p c t i", i=4))

        def quantize(u):
            w = UNITS[u]
            codes[u] = keep.tile([P, w], U32, name="codes%d" % u, align_bytes=64)
            scales[u] = keep.tile([P, w], U8, name="scales%d" % u, align_bytes=64)
            nc.vector.quantize_mx(out=codes[u][:].bitcast(FP8X4), scales=scales[u][:], in_=inter[u][:].rearrange("p c t -> p (c t)"))

        w3_codes = keep.tile([P, H], U32, name="w3_codes", align_bytes=64)
        w3_scales = keep.tile([P, H], U8, name="w3_scales", align_bytes=64)
        w3_grouped = keep.tile([P, H, T], BF16, name="w3_grouped", align_bytes=64)
        wc1_codes = keep.tile([P, H], U32, name="wc1_codes", align_bytes=64)
        wc1_scales = keep.tile([P, H], U8, name="wc1_scales", align_bytes=64)
        wc1_grouped = keep.tile([P, H, T], BF16, name="wc1_grouped", align_bytes=64)

        def quantize_weight(grouped, codes_t, scales_t):
            nc.vector.quantize_mx(out=codes_t[:].bitcast(FP8X4), scales=scales_t[:], in_=grouped[:].rearrange("p c j -> p (c j)"))

        def mm(dst, wc, ws, j, mc, ms):
            nc.tensor.matmul_mx(
                out=dst,
                lhsT=wc[:, 128 * j:128 * j + 128].bitcast(FP8X4),
                lhsT_scale=ws[:, 128 * j:128 * j + 128],
                rhs=mc.bitcast(FP8X4),
                rhs_scale=ms,
                start=True,
                stop=True,
            )

        def matmuls(u):
            w = UNITS[u]
            if starts[u] == 0:
                for j in range(T):
                    first_banks.append(bank())
            if starts[u] < 512:
                outs = [first_banks[j][:, starts[u]:starts[u] + w] for j in range(T)]
            else:
                outs = [bank()[:] for j in range(T)]
            for j in range(T):
                mm(outs[j], w3_codes, w3_scales, j, codes[u][:], scales[u][:])
            banks[u] = outs

        low = keep.tile([P, T, 512], F32, name="low", align_bytes=64)
        lowb = keep.tile([P, T, 512], BF16, name="lowb", align_bytes=64)
        top = keep.tile([P, AS, 512], BF16, name="top", align_bytes=64)

        def empty_scalar(u):
            if u < AT:
                return
            if u == AT:
                fresh[u] = top
            else:
                fresh[u] = keep.tile([P, AS, UNITS[u]], BF16, name="fresh%d" % u, align_bytes=64)
            for j in range(AS):
                nc.scalar.activation(out=fresh[u][:, j, :], in_=banks[u][j], func=ACT.Relu, scale=a3[:, j:j + 1], bias=c3[:, j:j + 1])

        def finish_low(j):
            nc.scalar.activation(out=lowb[:, j, :], in_=low[:, j, :], func=ACT.Relu, bias=c3[:, j:j + 1])

        def empty_vector(u):
            for j in range(AS if u >= AT else 0, T):
                if starts[u] < 512:
                    nc.vector.tensor_scalar(out=low[:, j, :], in0=first_banks[j][:], scalar1=a3[:, j:j + 1], scalar2=None, op0=ALU.mult)
                else:
                    nc.vector.scalar_tensor_tensor(out=low[:, j, :], in0=banks[u][j], scalar=a3[:, j:j + 1], in1=low[:, j, :], op0=ALU.mult, op1=ALU.max)

        def tmax(dst, x, y):
            nc.vector.tensor_tensor(out=dst, in0=x, in1=y, op=ALU.max)

        for t in range(T):
            widen(0, t)
        for t in range(T):
            widen(1, t)
        bn_begin(0, "bn3")
        bn_root("bn3")
        xt3 = transpose_weight(w3_raw)
        spin(WARM[1])
        interleave(0, "v")
        interleave(1, "v")
        a3, c3 = bn_finish(0, "bn3")
        for hf in range(2):
            copy_weight(nc.scalar.copy if WCOPY[hf] == "s" else nc.vector.tensor_copy, w3_grouped, hf, xt3[hf])
        quantize(0)
        quantize_weight(w3_grouped, w3_codes, w3_scales)
        xtc = transpose_weight(wc1_raw)
        matmuls(0)
        quantize(1)
        matmuls(1)
        for t in range(T):
            widen(2, t)
        interleave(2, "g")
        interleave(2, "s")
        for t in range(T):
            widen(3, t)
        for hf in range(2):
            copy_weight(nc.scalar.copy if WCOPY[2 + hf] == "s" else nc.vector.tensor_copy, wc1_grouped, hf, xtc[hf])
        interleave(2, "v")

        last = n_units - 1
        for u in range(2, n_units):
            if u + 1 < n_units:
                interleave(u + 1, "v")
            quantize(u)
            matmuls(u)
            if u + 1 < n_units:
                ones[u + 1] = keep.tile([P, 1], F32, name="one%d" % u)
                nc.vector.memset(ones[u + 1][:], 1.0)
                interleave(u + 1, "g")
                interleave(u + 1, "s")
            if u + 2 < n_units:
                for t in range(T):
                    widen(u + 2, t)
            if u == 3:
                bn_begin(4, "bnc")
            if u == 4:
                bn_root("bnc")
            if u == BNC:
                ac, cc = bn_finish(4, "bnc")
            if u == QC:
                quantize_weight(wc1_grouped, wc1_codes, wc1_scales)
            empty_scalar(u - 1)
            empty_vector(u - 1)
            if u == AT:
                for j in range(AS):
                    finish_low(j)
        half = keep.tile([P, T, 256], BF16, name="half", align_bytes=64)
        other = keep.tile([P, AS, 256], BF16, name="other", align_bytes=64)
        pooled = keep.tile([P, N, T], BF16, name="pooled", align_bytes=64)

        def fold(dst, src):
            tmax(dst, src[:, :, 0:256], src[:, :, 256:512])

        empty_scalar(last)
        fold(half[:, 0:AS, :], lowb[:, 0:AS, :])
        fold(other[:], top)
        empty_vector(last)
        for j in range(AS, T):
            finish_low(j)
        tmax(half[:, 0:AS, :], half[:, 0:AS, :], other[:])
        fold(other[:], fresh[last])
        fold(half[:, 2:3, :], lowb[:, 2:3, :])
        tmax(half[:, 0:AS, :], half[:, 0:AS, :], other[:])
        fold(half[:, 3:4, :], lowb[:, 3:4, :])
        tmax(pooled[:], half[:, :, 0:128].rearrange("p j n -> p n j"), half[:, :, 128:256].rearrange("p j n -> p n j"))

        p_codes = keep.tile([P, N], U32, name="p_codes", align_bytes=64)
        p_scales = keep.tile([P, N], U8, name="p_scales", align_bytes=64)
        nc.vector.quantize_mx(out=p_codes[:].bitcast(FP8X4), scales=p_scales[:], in_=pooled[:].rearrange("p n j -> p (n j)"))
        result = keep.tile([P, T, N], F32, name="result", align_bytes=64)
        ys = [bank(), bank()]
        for j in range(T):
            mm(ys[j // 2][:, 256 * (j % 2):256 * (j % 2) + 128], wc1_codes, wc1_scales, j, p_codes[:], p_scales[:])
        for j in range(T):
            nc.scalar.activation(out=result[:, j, :], in_=ys[j // 2][:, 256 * (j % 2):256 * (j % 2) + 128], func=ACT.Relu, scale=ac[:, j:j + 1], bias=cc[:, j:j + 1])
        nc.sync.dma_start(out=out.rearrange("o (p t) n -> p (o t) n", t=T), in_=result[:])
